import numpy as np
import ml_dtypes

BF16 = ml_dtypes.bfloat16


def bf(x):
    return np.asarray(x, np.float32).astype(BF16)


def f32(x):
    return np.asarray(x, np.float32)


def f64(x):
    return np.asarray(x).astype(np.float64)


def striped(idx):
    return np.tile(idx.reshape(-1, 16).T, (8, 1))


C, S, H, N, K = 128, 2048, 512, 1024, 16

GATE = np.array([
    [0.0, 0.0, 0.0, 0.0],
    [0.0, 0.0, 0.0, 1.0],
    [0.0, 1.0, 0.0, -1.0],
    [0.0, 1.0, 0.0, 0.0],
    [0.0, 0.0, 1.0, -1.0],
    [0.0, 0.0, 1.0, 0.0],
    [0.0, 1.0, 1.0, -2.0],
    [0.0, 1.0, 1.0, -1.0],
    [1.0, -1.0, -1.0, 1.0],
    [1.0, -1.0, -1.0, 2.0],
    [1.0, 0.0, -1.0, 0.0],
    [1.0, 0.0, -1.0, 1.0],
    [1.0, -1.0, 0.0, 0.0],
    [1.0, -1.0, 0.0, 1.0],
    [1.0, 0.0, 0.0, -1.0],
    [1.0, 0.0, 0.0, 0.0],
], np.float64)


def setup_inputs():
    return {"x": f32(np.random.random((C, S)) > 0.5), "w": f32(np.random.standard_normal((K, H))), "offs": striped(np.random.permutation(np.tile(np.arange(S), 2))[:N])}


def reference(x, w, offs):
    idx = offs[:16].T.reshape(-1)
    e = np.exp(f64(w))
    p = e / e.sum(axis=0, keepdims=True)
    k = (GATE[:, :, None] * p[:, None, :]).sum(axis=0)
    a = f64(x)[:, idx[:H]]
    b = f64(x)[:, idx[H:]]
    return k[0] + k[1] * a + k[2] * b + k[3] * (a * b)

@@ -1,0 +1,104 @@
+import concourse.mybir as mybir
+from concourse.masks import make_identity
+
+F32 = mybir.dt.float32
+U16 = mybir.dt.uint16
+ALU = mybir.AluOpType
+ACT = mybir.ActivationFunctionType
+AXIS = mybir.AxisListType
+
+P = 128
+INPUTS = 2048
+NEURONS = 512
+GATES = 16
+BLOCKS = NEURONS // P
+LIST_COLS = NEURONS // 16
+SUMS = 5
+
+
+def tile_tanklogicvaluenetwork_kernel(tc, x, w, offs, out):
+    nc = tc.nc
+    with (
+        tc.tile_pool(name="held", bufs=1) as held,
+        tc.psum_pool(name="psum", bufs=1) as psum,
+    ):
+        offsets = held.tile([P, 2 * LIST_COLS], U16, name="offsets")
+        nc.sync.dma_start(offsets[:], offs)
+        w_rows = held.tile([GATES, NEURONS], F32, name="w_rows")
+        nc.scalar.dma_start(w_rows[:], w)
+        table = held.tile([P, INPUTS], F32, name="table")
+        nc.sync.dma_start(table[:], x)
+
+        identity = held.tile([P, P], F32, name="identity")
+        make_identity(nc, identity[:])
+
+        gate = held.tile([P, SUMS, GATES], F32, name="gate")
+        nc.vector.memset(gate[:, 0:4, :], 0.0)
+        nc.vector.memset(gate[:, 4, :], 1.0)
+        for row, bit in ((0, 3), (1, 1), (2, 2), (3, 0)):
+            where_set = gate[:, row, :].rearrange("p (h two f) -> p h two f", two=2, f=2**bit)
+            nc.vector.memset(where_set[:, :, 1, :], 1.0)
+        bit3_twice = gate[:, 0:1, :].to_broadcast([P, 2, GATES])
+        nc.vector.tensor_sub(gate[:, 3, :], gate[:, 3, :], gate[:, 1, :])
+        nc.vector.tensor_sub(gate[:, 1:3, :], gate[:, 1:3, :], bit3_twice)
+        nc.vector.tensor_sub(gate[:, 3, :], gate[:, 3, :], gate[:, 2, :])
+
+        w_cols = psum.tile([P, BLOCKS, GATES], F32, name="w_cols")
+        for blk in range(BLOCKS):
+            nc.tensor.matmul(
+                w_cols[:, blk, :],
+                w_rows[:, blk * P : (blk + 1) * P],
+                identity[0:GATES, 0:GATES],
+                start=True,
+                stop=True,
+            )
+        top = held.tile([P, BLOCKS], F32, name="top")
+        nc.vector.reduce_max(top[:], w_cols[:], axis=AXIS.X)
+        shifted = held.tile([P, BLOCKS, GATES], F32, name="shifted")
+        nc.vector.tensor_sub(
+            shifted[:], w_cols[:], top[:].unsqueeze(2).to_broadcast([P, BLOCKS, GATES])
+        )
+        weight = held.tile([P, BLOCKS, GATES], F32, name="weight")
+        nc.scalar.activation(weight[:], shifted[:], ACT.Exp)
+
+        shape = [P, BLOCKS, SUMS, GATES]
+        weighted = held.tile(shape, F32, name="weighted")
+        nc.vector.tensor_mul(
+            weighted[:],
+            weight[:].unsqueeze(2).to_broadcast(shape),
+            gate[:].unsqueeze(1).to_broadcast(shape),
+        )
+        sums = held.tile([P, BLOCKS, SUMS], F32, name="sums")
+        nc.vector.reduce_sum(sums[:], weighted[:], axis=AXIS.X)
+        inverse = held.tile([P, BLOCKS, 1], F32, name="inverse")
+        nc.vector.reciprocal(inverse[:], sums[:, :, 4:5])
+        coef = held.tile([P, BLOCKS, 4], F32, name="coef")
+        nc.vector.tensor_mul(coef[:], sums[:, :, 0:4], inverse[:].to_broadcast([P, BLOCKS, 4]))
+
+        k_rows = {}
+        for i in (3, 2, 1, 0):
+            k_bank = psum.tile([P, NEURONS], F32, name=f"k{i}_bank")
+            for blk in range(BLOCKS):
+                nc.tensor.transpose(
+                    k_bank[:, blk * P : (blk + 1) * P],
+                    coef[:, blk, i : i + 1].to_broadcast([P, P]),
+                    identity[:],
+                )
+            k_rows[i] = held.tile([P, NEURONS], F32, name=f"k{i}_rows")
+            nc.scalar.copy(k_rows[i][:], k_bank[:])
+
+        first_inputs = offsets[:, 0:LIST_COLS]
+        second_inputs = offsets[:, LIST_COLS : 2 * LIST_COLS]
+
+        slope = held.tile([P, NEURONS], F32, name="slope")
+        nc.vector.tensor_tensor(slope[:], table[:].indirect(second_inputs), k_rows[3][:], ALU.mult)
+        nc.vector.tensor_add(slope[:], slope[:], k_rows[1][:])
+
+        base = held.tile([P, NEURONS], F32, name="base")
+        nc.vector.tensor_tensor(base[:], table[:].indirect(second_inputs), k_rows[2][:], ALU.mult)
+        nc.vector.tensor_add(base[:], base[:], k_rows[0][:])
+
+        result = held.tile([P, NEURONS], F32, name="result")
+        nc.vector.tensor_tensor(result[:], table[:].indirect(first_inputs), slope[:], ALU.mult)
+        nc.vector.tensor_add(result[:], result[:], base[:])
+        nc.sync.dma_start(out, result[:])

@@ -13,6 +13,7 @@ NEURONS = 512
 GATES = 16
 BLOCKS = NEURONS // P
 LIST_COLS = NEURONS // 16
+HALVES = (slice(0, NEURONS // 2), slice(NEURONS // 2, NEURONS))
 SUMS = 5
 
 
@@ -75,30 +76,36 @@ def tile_tanklogicvaluenetwork_kernel(tc, x, w, offs, out):
         coef = held.tile([P, BLOCKS, 4], F32, name="coef")
         nc.vector.tensor_mul(coef[:], sums[:, :, 0:4], inverse[:].to_broadcast([P, BLOCKS, 4]))
 
-        k_rows = {}
-        for i in (3, 2, 1, 0):
-            k_bank = psum.tile([P, NEURONS], F32, name=f"k{i}_bank")
+        k_bank = {}
+        for i in (3, 1, 2, 0):
+            k_bank[i] = psum.tile([P, NEURONS], F32, name=f"k{i}_bank")
             for blk in range(BLOCKS):
                 nc.tensor.transpose(
-                    k_bank[:, blk * P : (blk + 1) * P],
+                    k_bank[i][:, blk * P : (blk + 1) * P],
                     coef[:, blk, i : i + 1].to_broadcast([P, P]),
                     identity[:],
                 )
+        k_rows = {}
+        for i in (3, 2):
             k_rows[i] = held.tile([P, NEURONS], F32, name=f"k{i}_rows")
-            nc.scalar.copy(k_rows[i][:], k_bank[:])
+            for half in HALVES:
+                nc.scalar.copy(k_rows[i][:, half], k_bank[i][:, half])
 
         first_inputs = offsets[:, 0:LIST_COLS]
         second_inputs = offsets[:, LIST_COLS : 2 * LIST_COLS]
 
         slope = held.tile([P, NEURONS], F32, name="slope")
-        nc.vector.tensor_tensor(slope[:], table[:].indirect(second_inputs), k_rows[3][:], ALU.mult)
-        nc.vector.tensor_add(slope[:], slope[:], k_rows[1][:])
-
-        base = held.tile([P, NEURONS], F32, name="base")
-        nc.vector.tensor_tensor(base[:], table[:].indirect(second_inputs), k_rows[2][:], ALU.mult)
-        nc.vector.tensor_add(base[:], base[:], k_rows[0][:])
+        for n, half in enumerate(HALVES):
+            piece = offsets[:, LIST_COLS + n * LIST_COLS // 2 : LIST_COLS + (n + 1) * LIST_COLS // 2]
+            nc.vector.tensor_tensor(slope[:, half], table[:].indirect(piece), k_rows[3][:, half], ALU.mult)
+        nc.vector.tensor_add(slope[:], slope[:], k_bank[1][:])
 
         result = held.tile([P, NEURONS], F32, name="result")
         nc.vector.tensor_tensor(result[:], table[:].indirect(first_inputs), slope[:], ALU.mult)
+
+        base = held.tile([P, NEURONS], F32, name="base")
+        nc.vector.tensor_tensor(base[:], table[:].indirect(second_inputs), k_rows[2][:], ALU.mult)
+        nc.vector.tensor_add(base[:], base[:], k_bank[0][:])
+
         nc.vector.tensor_add(result[:], result[:], base[:])
         nc.sync.dma_start(out, result[:])

@@ -13,7 +13,7 @@ NEURONS = 512
 GATES = 16
 BLOCKS = NEURONS // P
 LIST_COLS = NEURONS // 16
-HALVES = (slice(0, NEURONS // 2), slice(NEURONS // 2, NEURONS))
+HALF = NEURONS // 2
 SUMS = 5
 
 
@@ -25,8 +25,8 @@ def tile_tanklogicvaluenetwork_kernel(tc, x, w, offs, out):
     ):
         offsets = held.tile([P, 2 * LIST_COLS], U16, name="offsets")
         nc.sync.dma_start(offsets[:], offs)
-        w_rows = held.tile([GATES, NEURONS], F32, name="w_rows")
-        nc.scalar.dma_start(w_rows[:], w)
+        w_rows = held.tile([GATES * BLOCKS, P], F32, name="w_rows")
+        nc.scalar.dma_start(w_rows[:], w.rearrange("q (blk n) -> (q blk) n", n=P))
         table = held.tile([P, INPUTS], F32, name="table")
         nc.sync.dma_start(table[:], x)
 
@@ -44,20 +44,14 @@ def tile_tanklogicvaluenetwork_kernel(tc, x, w, offs, out):
         nc.vector.tensor_sub(gate[:, 1:3, :], gate[:, 1:3, :], bit3_twice)
         nc.vector.tensor_sub(gate[:, 3, :], gate[:, 3, :], gate[:, 2, :])
 
-        w_cols = psum.tile([P, BLOCKS, GATES], F32, name="w_cols")
-        for blk in range(BLOCKS):
-            nc.tensor.matmul(
-                w_cols[:, blk, :],
-                w_rows[:, blk * P : (blk + 1) * P],
-                identity[0:GATES, 0:GATES],
-                start=True,
-                stop=True,
-            )
+        w_bank = psum.tile([P, GATES * BLOCKS], F32, name="w_bank")
+        nc.tensor.transpose(w_bank[:], w_rows[:], identity[0 : GATES * BLOCKS, 0 : GATES * BLOCKS])
+        w_cols = w_bank[:].rearrange("p (q blk) -> p blk q", blk=BLOCKS)
         top = held.tile([P, BLOCKS], F32, name="top")
-        nc.vector.reduce_max(top[:], w_cols[:], axis=AXIS.X)
+        nc.vector.reduce_max(top[:], w_cols, axis=AXIS.X)
         shifted = held.tile([P, BLOCKS, GATES], F32, name="shifted")
         nc.vector.tensor_sub(
-            shifted[:], w_cols[:], top[:].unsqueeze(2).to_broadcast([P, BLOCKS, GATES])
+            shifted[:], w_cols, top[:].unsqueeze(2).to_broadcast([P, BLOCKS, GATES])
         )
         weight = held.tile([P, BLOCKS, GATES], F32, name="weight")
         nc.scalar.activation(weight[:], shifted[:], ACT.Exp)
@@ -77,7 +71,7 @@ def tile_tanklogicvaluenetwork_kernel(tc, x, w, offs, out):
         nc.vector.tensor_mul(coef[:], sums[:, :, 0:4], inverse[:].to_broadcast([P, BLOCKS, 4]))
 
         k_bank = {}
-        for i in (3, 1, 2, 0):
+        for i in (3, 2, 1, 0):
             k_bank[i] = psum.tile([P, NEURONS], F32, name=f"k{i}_bank")
             for blk in range(BLOCKS):
                 nc.tensor.transpose(
@@ -85,27 +79,21 @@ def tile_tanklogicvaluenetwork_kernel(tc, x, w, offs, out):
                     coef[:, blk, i : i + 1].to_broadcast([P, P]),
                     identity[:],
                 )
-        k_rows = {}
-        for i in (3, 2):
-            k_rows[i] = held.tile([P, NEURONS], F32, name=f"k{i}_rows")
-            for half in HALVES:
-                nc.scalar.copy(k_rows[i][:, half], k_bank[i][:, half])
+        k3_rows = held.tile([P, NEURONS], F32, name="k3_rows")
+        nc.scalar.copy(k3_rows[:, 0:HALF], k_bank[3][:, 0:HALF])
+        nc.vector.tensor_copy(k3_rows[:, HALF:NEURONS], k_bank[3][:, HALF:NEURONS])
+        k2_rows = held.tile([P, NEURONS], F32, name="k2_rows")
+        nc.scalar.copy(k2_rows[:], k_bank[2][:])
 
         first_inputs = offsets[:, 0:LIST_COLS]
         second_inputs = offsets[:, LIST_COLS : 2 * LIST_COLS]
-
         slope = held.tile([P, NEURONS], F32, name="slope")
-        for n, half in enumerate(HALVES):
-            piece = offsets[:, LIST_COLS + n * LIST_COLS // 2 : LIST_COLS + (n + 1) * LIST_COLS // 2]
-            nc.vector.tensor_tensor(slope[:, half], table[:].indirect(piece), k_rows[3][:, half], ALU.mult)
-        nc.vector.tensor_add(slope[:], slope[:], k_bank[1][:])
-
-        result = held.tile([P, NEURONS], F32, name="result")
-        nc.vector.tensor_tensor(result[:], table[:].indirect(first_inputs), slope[:], ALU.mult)
-
         base = held.tile([P, NEURONS], F32, name="base")
-        nc.vector.tensor_tensor(base[:], table[:].indirect(second_inputs), k_rows[2][:], ALU.mult)
+        result = held.tile([P, NEURONS], F32, name="result")
+        nc.vector.tensor_tensor(slope[:], table[:].indirect(second_inputs), k3_rows[:], ALU.mult)
+        nc.vector.tensor_tensor(base[:], table[:].indirect(second_inputs), k2_rows[:], ALU.mult)
+        nc.vector.tensor_add(slope[:], slope[:], k_bank[1][:])
         nc.vector.tensor_add(base[:], base[:], k_bank[0][:])
-
+        nc.vector.tensor_tensor(result[:], table[:].indirect(first_inputs), slope[:], ALU.mult)
         nc.vector.tensor_add(result[:], result[:], base[:])
         nc.sync.dma_start(out, result[:])

@@ -14,7 +14,7 @@ GATES = 16
 BLOCKS = NEURONS // P
 LIST_COLS = NEURONS // 16
 HALF = NEURONS // 2
-SUMS = 5
+COEFS = 4
 
 
 def tile_tanklogicvaluenetwork_kernel(tc, x, w, offs, out):
@@ -23,19 +23,18 @@ def tile_tanklogicvaluenetwork_kernel(tc, x, w, offs, out):
         tc.tile_pool(name="held", bufs=1) as held,
         tc.psum_pool(name="psum", bufs=1) as psum,
     ):
+        w_rows = held.tile([GATES * BLOCKS, P], F32, name="w_rows")
+        nc.sync.dma_start(w_rows[:], w.rearrange("q (blk n) -> (q blk) n", n=P))
         offsets = held.tile([P, 2 * LIST_COLS], U16, name="offsets")
         nc.sync.dma_start(offsets[:], offs)
-        w_rows = held.tile([GATES * BLOCKS, P], F32, name="w_rows")
-        nc.scalar.dma_start(w_rows[:], w.rearrange("q (blk n) -> (q blk) n", n=P))
         table = held.tile([P, INPUTS], F32, name="table")
-        nc.sync.dma_start(table[:], x)
+        nc.scalar.dma_start(table[:], x)
 
         identity = held.tile([P, P], F32, name="identity")
         make_identity(nc, identity[:])
 
-        gate = held.tile([P, SUMS, GATES], F32, name="gate")
-        nc.vector.memset(gate[:, 0:4, :], 0.0)
-        nc.vector.memset(gate[:, 4, :], 1.0)
+        gate = held.tile([P, COEFS, GATES], F32, name="gate")
+        nc.vector.memset(gate[:], 0.0)
         for row, bit in ((0, 3), (1, 1), (2, 2), (3, 0)):
             where_set = gate[:, row, :].rearrange("p (h two f) -> p h two f", two=2, f=2**bit)
             nc.vector.memset(where_set[:, :, 1, :], 1.0)
@@ -56,19 +55,21 @@ def tile_tanklogicvaluenetwork_kernel(tc, x, w, offs, out):
         weight = held.tile([P, BLOCKS, GATES], F32, name="weight")
         nc.scalar.activation(weight[:], shifted[:], ACT.Exp)
 
-        shape = [P, BLOCKS, SUMS, GATES]
+        shape = [P, BLOCKS, COEFS, GATES]
+        total = held.tile([P, BLOCKS, 1], F32, name="total")
+        nc.vector.reduce_sum(total[:], weight[:], axis=AXIS.X)
         weighted = held.tile(shape, F32, name="weighted")
         nc.vector.tensor_mul(
             weighted[:],
             weight[:].unsqueeze(2).to_broadcast(shape),
             gate[:].unsqueeze(1).to_broadcast(shape),
         )
-        sums = held.tile([P, BLOCKS, SUMS], F32, name="sums")
-        nc.vector.reduce_sum(sums[:], weighted[:], axis=AXIS.X)
         inverse = held.tile([P, BLOCKS, 1], F32, name="inverse")
-        nc.vector.reciprocal(inverse[:], sums[:, :, 4:5])
-        coef = held.tile([P, BLOCKS, 4], F32, name="coef")
-        nc.vector.tensor_mul(coef[:], sums[:, :, 0:4], inverse[:].to_broadcast([P, BLOCKS, 4]))
+        nc.vector.reciprocal(inverse[:], total[:])
+        sums = held.tile([P, BLOCKS, COEFS], F32, name="sums")
+        nc.vector.reduce_sum(sums[:], weighted[:], axis=AXIS.X)
+        coef = held.tile([P, BLOCKS, COEFS], F32, name="coef")
+        nc.vector.tensor_mul(coef[:], sums[:], inverse[:].to_broadcast([P, BLOCKS, COEFS]))
 
         k_bank = {}
         for i in (3, 2, 1, 0):

@@ -72,29 +72,32 @@ def tile_tanklogicvaluenetwork_kernel(tc, x, w, offs, out):
         nc.vector.tensor_mul(coef[:], sums[:], inverse[:].to_broadcast([P, BLOCKS, COEFS]))
 
         k_bank = {}
-        for i in (3, 2, 1, 0):
+        for i in (2, 3, 1, 0):
             k_bank[i] = psum.tile([P, NEURONS], F32, name=f"k{i}_bank")
             for blk in range(BLOCKS):
-                nc.tensor.transpose(
+                nc.tensor.matmul(
                     k_bank[i][:, blk * P : (blk + 1) * P],
                     coef[:, blk, i : i + 1].to_broadcast([P, P]),
                     identity[:],
+                    is_transpose=True,
+                    start=(blk == 0),
+                    stop=(blk == BLOCKS - 1 and i != 0),
                 )
-        k3_rows = held.tile([P, NEURONS], F32, name="k3_rows")
-        nc.scalar.copy(k3_rows[:, 0:HALF], k_bank[3][:, 0:HALF])
-        nc.vector.tensor_copy(k3_rows[:, HALF:NEURONS], k_bank[3][:, HALF:NEURONS])
         k2_rows = held.tile([P, NEURONS], F32, name="k2_rows")
-        nc.scalar.copy(k2_rows[:], k_bank[2][:])
+        nc.scalar.copy(k2_rows[:, 0:HALF], k_bank[2][:, 0:HALF])
+        nc.vector.tensor_copy(k2_rows[:, HALF:NEURONS], k_bank[2][:, HALF:NEURONS])
+        k3_rows = held.tile([P, NEURONS], F32, name="k3_rows")
+        nc.scalar.copy(k3_rows[:], k_bank[3][:])
 
         first_inputs = offsets[:, 0:LIST_COLS]
         second_inputs = offsets[:, LIST_COLS : 2 * LIST_COLS]
+        k2_b = held.tile([P, NEURONS], F32, name="k2_b")
         slope = held.tile([P, NEURONS], F32, name="slope")
-        base = held.tile([P, NEURONS], F32, name="base")
         result = held.tile([P, NEURONS], F32, name="result")
+        nc.vector.tensor_tensor(k2_b[:], table[:].indirect(second_inputs), k2_rows[:], ALU.mult)
+        nc.tensor.matmul(k_bank[0][:], identity[:], k2_b[:], start=False, stop=True)
         nc.vector.tensor_tensor(slope[:], table[:].indirect(second_inputs), k3_rows[:], ALU.mult)
-        nc.vector.tensor_tensor(base[:], table[:].indirect(second_inputs), k2_rows[:], ALU.mult)
         nc.vector.tensor_add(slope[:], slope[:], k_bank[1][:])
-        nc.vector.tensor_add(base[:], base[:], k_bank[0][:])
         nc.vector.tensor_tensor(result[:], table[:].indirect(first_inputs), slope[:], ALU.mult)
-        nc.vector.tensor_add(result[:], result[:], base[:])
+        nc.vector.tensor_add(result[:], result[:], k_bank[0][:])
         nc.sync.dma_start(out, result[:])

@@ -13,7 +13,6 @@ NEURONS = 512
 GATES = 16
 BLOCKS = NEURONS // P
 LIST_COLS = NEURONS // 16
-HALF = NEURONS // 2
 COEFS = 4
 
 
@@ -55,49 +54,51 @@ def tile_tanklogicvaluenetwork_kernel(tc, x, w, offs, out):
         weight = held.tile([P, BLOCKS, GATES], F32, name="weight")
         nc.scalar.activation(weight[:], shifted[:], ACT.Exp)
 
-        shape = [P, BLOCKS, COEFS, GATES]
         total = held.tile([P, BLOCKS, 1], F32, name="total")
         nc.vector.reduce_sum(total[:], weight[:], axis=AXIS.X)
+        r_col = held.tile([P, BLOCKS, 1], F32, name="r_col")
+        nc.vector.reciprocal(r_col[:], total[:])
+        shape = [P, BLOCKS, COEFS, GATES]
         weighted = held.tile(shape, F32, name="weighted")
         nc.vector.tensor_mul(
             weighted[:],
             weight[:].unsqueeze(2).to_broadcast(shape),
             gate[:].unsqueeze(1).to_broadcast(shape),
         )
-        inverse = held.tile([P, BLOCKS, 1], F32, name="inverse")
-        nc.vector.reciprocal(inverse[:], total[:])
-        sums = held.tile([P, BLOCKS, COEFS], F32, name="sums")
-        nc.vector.reduce_sum(sums[:], weighted[:], axis=AXIS.X)
-        coef = held.tile([P, BLOCKS, COEFS], F32, name="coef")
-        nc.vector.tensor_mul(coef[:], sums[:], inverse[:].to_broadcast([P, BLOCKS, COEFS]))
+        n_col = held.tile([P, BLOCKS, COEFS], F32, name="n_col")
+        nc.vector.reduce_sum(n_col[:], weighted[:], axis=AXIS.X)
+        k_col = held.tile([P, BLOCKS, 2], F32, name="k_col")
+        nc.vector.tensor_mul(k_col[:], n_col[:, :, 0:2], r_col[:].to_broadcast([P, BLOCKS, 2]))
 
-        k_bank = {}
-        for i in (2, 3, 1, 0):
-            k_bank[i] = psum.tile([P, NEURONS], F32, name=f"k{i}_bank")
+        def as_row(name, columns):
+            bank = psum.tile([P, NEURONS], F32, name=name)
             for blk in range(BLOCKS):
-                nc.tensor.matmul(
-                    k_bank[i][:, blk * P : (blk + 1) * P],
-                    coef[:, blk, i : i + 1].to_broadcast([P, P]),
+                nc.tensor.transpose(
+                    bank[:, blk * P : (blk + 1) * P],
+                    columns[:, blk : blk + 1].to_broadcast([P, P]),
                     identity[:],
-                    is_transpose=True,
-                    start=(blk == 0),
-                    stop=(blk == BLOCKS - 1 and i != 0),
                 )
-        k2_rows = held.tile([P, NEURONS], F32, name="k2_rows")
-        nc.scalar.copy(k2_rows[:, 0:HALF], k_bank[2][:, 0:HALF])
-        nc.vector.tensor_copy(k2_rows[:, HALF:NEURONS], k_bank[2][:, HALF:NEURONS])
-        k3_rows = held.tile([P, NEURONS], F32, name="k3_rows")
-        nc.scalar.copy(k3_rows[:], k_bank[3][:])
+            return bank
+
+        r_bank = as_row("r_bank", r_col[:, :, 0])
+        n3_bank = as_row("n3_bank", n_col[:, :, 3])
+        k1_bank = as_row("k1_bank", k_col[:, :, 1])
+        n2_bank = as_row("n2_bank", n_col[:, :, 2])
+        k0_bank = as_row("k0_bank", k_col[:, :, 0])
+        r_rows = held.tile([P, NEURONS], F32, name="r_rows")
+        nc.vector.tensor_copy(r_rows[:], r_bank[:])
 
         first_inputs = offsets[:, 0:LIST_COLS]
         second_inputs = offsets[:, LIST_COLS : 2 * LIST_COLS]
-        k2_b = held.tile([P, NEURONS], F32, name="k2_b")
+        r_b = held.tile([P, NEURONS], F32, name="r_b")
         slope = held.tile([P, NEURONS], F32, name="slope")
+        base = held.tile([P, NEURONS], F32, name="base")
         result = held.tile([P, NEURONS], F32, name="result")
-        nc.vector.tensor_tensor(k2_b[:], table[:].indirect(second_inputs), k2_rows[:], ALU.mult)
-        nc.tensor.matmul(k_bank[0][:], identity[:], k2_b[:], start=False, stop=True)
-        nc.vector.tensor_tensor(slope[:], table[:].indirect(second_inputs), k3_rows[:], ALU.mult)
-        nc.vector.tensor_add(slope[:], slope[:], k_bank[1][:])
+        nc.vector.tensor_tensor(r_b[:], table[:].indirect(second_inputs), r_rows[:], ALU.mult)
+        nc.vector.tensor_mul(slope[:], r_b[:], n3_bank[:])
+        nc.vector.tensor_add(slope[:], slope[:], k1_bank[:])
         nc.vector.tensor_tensor(result[:], table[:].indirect(first_inputs), slope[:], ALU.mult)
-        nc.vector.tensor_add(result[:], result[:], k_bank[0][:])
+        nc.vector.tensor_mul(base[:], r_b[:], n2_bank[:])
+        nc.vector.tensor_add(base[:], base[:], k0_bank[:])
+        nc.vector.tensor_add(result[:], result[:], base[:])
         nc.sync.dma_start(out, result[:])

@@ -81,24 +81,26 @@ def tile_tanklogicvaluenetwork_kernel(tc, x, w, offs, out):
             return bank
 
         r_bank = as_row("r_bank", r_col[:, :, 0])
+        n2_bank = as_row("n2_bank", n_col[:, :, 2])
         n3_bank = as_row("n3_bank", n_col[:, :, 3])
         k1_bank = as_row("k1_bank", k_col[:, :, 1])
-        n2_bank = as_row("n2_bank", n_col[:, :, 2])
         k0_bank = as_row("k0_bank", k_col[:, :, 0])
         r_rows = held.tile([P, NEURONS], F32, name="r_rows")
         nc.vector.tensor_copy(r_rows[:], r_bank[:])
+        n2_rows = held.tile([P, NEURONS], F32, name="n2_rows")
+        nc.scalar.copy(n2_rows[:], n2_bank[:])
 
         first_inputs = offsets[:, 0:LIST_COLS]
         second_inputs = offsets[:, LIST_COLS : 2 * LIST_COLS]
         r_b = held.tile([P, NEURONS], F32, name="r_b")
+        k2_b = held.tile([P, NEURONS], F32, name="k2_b")
         slope = held.tile([P, NEURONS], F32, name="slope")
-        base = held.tile([P, NEURONS], F32, name="base")
         result = held.tile([P, NEURONS], F32, name="result")
         nc.vector.tensor_tensor(r_b[:], table[:].indirect(second_inputs), r_rows[:], ALU.mult)
+        nc.gpsimd.tensor_mul(k2_b[:], r_b[:], n2_rows[:])
         nc.vector.tensor_mul(slope[:], r_b[:], n3_bank[:])
         nc.vector.tensor_add(slope[:], slope[:], k1_bank[:])
         nc.vector.tensor_tensor(result[:], table[:].indirect(first_inputs), slope[:], ALU.mult)
-        nc.vector.tensor_mul(base[:], r_b[:], n2_bank[:])
-        nc.vector.tensor_add(base[:], base[:], k0_bank[:])
-        nc.vector.tensor_add(result[:], result[:], base[:])
+        nc.vector.tensor_add(result[:], result[:], k0_bank[:])
+        nc.vector.tensor_add(result[:], result[:], k2_b[:])
         nc.sync.dma_start(out, result[:])

@@ -27,7 +27,7 @@ def tile_tanklogicvaluenetwork_kernel(tc, x, w, offs, out):
         offsets = held.tile([P, 2 * LIST_COLS], U16, name="offsets")
         nc.sync.dma_start(offsets[:], offs)
         table = held.tile([P, INPUTS], F32, name="table")
-        nc.scalar.dma_start(table[:], x)
+        nc.sync.dma_start(table[:], x)
 
         identity = held.tile([P, P], F32, name="identity")
         make_identity(nc, identity[:])
@@ -81,26 +81,24 @@ def tile_tanklogicvaluenetwork_kernel(tc, x, w, offs, out):
             return bank
 
         r_bank = as_row("r_bank", r_col[:, :, 0])
-        n2_bank = as_row("n2_bank", n_col[:, :, 2])
         n3_bank = as_row("n3_bank", n_col[:, :, 3])
         k1_bank = as_row("k1_bank", k_col[:, :, 1])
+        n2_bank = as_row("n2_bank", n_col[:, :, 2])
         k0_bank = as_row("k0_bank", k_col[:, :, 0])
         r_rows = held.tile([P, NEURONS], F32, name="r_rows")
         nc.vector.tensor_copy(r_rows[:], r_bank[:])
-        n2_rows = held.tile([P, NEURONS], F32, name="n2_rows")
-        nc.scalar.copy(n2_rows[:], n2_bank[:])
 
         first_inputs = offsets[:, 0:LIST_COLS]
         second_inputs = offsets[:, LIST_COLS : 2 * LIST_COLS]
         r_b = held.tile([P, NEURONS], F32, name="r_b")
-        k2_b = held.tile([P, NEURONS], F32, name="k2_b")
         slope = held.tile([P, NEURONS], F32, name="slope")
+        base = held.tile([P, NEURONS], F32, name="base")
         result = held.tile([P, NEURONS], F32, name="result")
         nc.vector.tensor_tensor(r_b[:], table[:].indirect(second_inputs), r_rows[:], ALU.mult)
-        nc.gpsimd.tensor_mul(k2_b[:], r_b[:], n2_rows[:])
         nc.vector.tensor_mul(slope[:], r_b[:], n3_bank[:])
         nc.vector.tensor_add(slope[:], slope[:], k1_bank[:])
         nc.vector.tensor_tensor(result[:], table[:].indirect(first_inputs), slope[:], ALU.mult)
-        nc.vector.tensor_add(result[:], result[:], k0_bank[:])
-        nc.vector.tensor_add(result[:], result[:], k2_b[:])
+        nc.vector.tensor_mul(base[:], r_b[:], n2_bank[:])
+        nc.vector.tensor_add(base[:], base[:], k0_bank[:])
+        nc.vector.tensor_add(result[:], result[:], base[:])
         nc.sync.dma_start(out, result[:])

@@ -14,6 +14,7 @@ GATES = 16
 BLOCKS = NEURONS // P
 LIST_COLS = NEURONS // 16
 COEFS = 4
+HALF = NEURONS // 2
 
 
 def tile_tanklogicvaluenetwork_kernel(tc, x, w, offs, out):
@@ -82,23 +83,38 @@ def tile_tanklogicvaluenetwork_kernel(tc, x, w, offs, out):
 
         r_bank = as_row("r_bank", r_col[:, :, 0])
         n3_bank = as_row("n3_bank", n_col[:, :, 3])
-        k1_bank = as_row("k1_bank", k_col[:, :, 1])
         n2_bank = as_row("n2_bank", n_col[:, :, 2])
+        k1_bank = as_row("k1_bank", k_col[:, :, 1])
         k0_bank = as_row("k0_bank", k_col[:, :, 0])
-        r_rows = held.tile([P, NEURONS], F32, name="r_rows")
-        nc.vector.tensor_copy(r_rows[:], r_bank[:])
 
-        first_inputs = offsets[:, 0:LIST_COLS]
-        second_inputs = offsets[:, LIST_COLS : 2 * LIST_COLS]
+        r_rows = held.tile([P, NEURONS], F32, name="r_rows")
         r_b = held.tile([P, NEURONS], F32, name="r_b")
         slope = held.tile([P, NEURONS], F32, name="slope")
         base = held.tile([P, NEURONS], F32, name="base")
+        a_slope = held.tile([P, NEURONS], F32, name="a_slope")
         result = held.tile([P, NEURONS], F32, name="result")
-        nc.vector.tensor_tensor(r_b[:], table[:].indirect(second_inputs), r_rows[:], ALU.mult)
-        nc.vector.tensor_mul(slope[:], r_b[:], n3_bank[:])
-        nc.vector.tensor_add(slope[:], slope[:], k1_bank[:])
-        nc.vector.tensor_tensor(result[:], table[:].indirect(first_inputs), slope[:], ALU.mult)
-        nc.vector.tensor_mul(base[:], r_b[:], n2_bank[:])
-        nc.vector.tensor_add(base[:], base[:], k0_bank[:])
-        nc.vector.tensor_add(result[:], result[:], base[:])
-        nc.sync.dma_start(out, result[:])
+        halves = [slice(h * HALF, (h + 1) * HALF) for h in range(2)]
+
+        def list_columns(first_entry, half):
+            start = (first_entry + half.start) // 16
+            return offsets[:, start : start + HALF // 16]
+
+        for half in halves:
+            nc.vector.tensor_copy(r_rows[:, half], r_bank[:, half])
+        for half in halves:
+            second_inputs = table[:].indirect(list_columns(NEURONS, half))
+            nc.vector.tensor_tensor(r_b[:, half], second_inputs, r_rows[:, half], ALU.mult)
+        for half in halves:
+            nc.vector.tensor_mul(slope[:, half], r_b[:, half], n3_bank[:, half])
+        for half in halves:
+            nc.vector.tensor_mul(base[:, half], r_b[:, half], n2_bank[:, half])
+        for half in halves:
+            nc.vector.tensor_add(slope[:, half], slope[:, half], k1_bank[:, half])
+        for half in halves:
+            nc.vector.tensor_add(base[:, half], base[:, half], k0_bank[:, half])
+        for half in halves:
+            first_inputs = table[:].indirect(list_columns(0, half))
+            nc.vector.tensor_tensor(a_slope[:, half], first_inputs, slope[:, half], ALU.mult)
+        for half in halves:
+            nc.vector.tensor_add(result[:, half], a_slope[:, half], base[:, half])
+            nc.sync.dma_start(out[:, half], result[:, half])

@@ -46,17 +46,19 @@ def tile_tanklogicvaluenetwork_kernel(tc, x, w, offs, out):
         w_bank = psum.tile([P, GATES * BLOCKS], F32, name="w_bank")
         nc.tensor.transpose(w_bank[:], w_rows[:], identity[0 : GATES * BLOCKS, 0 : GATES * BLOCKS])
         w_cols = w_bank[:].rearrange("p (q blk) -> p blk q", blk=BLOCKS)
-        top = held.tile([P, BLOCKS], F32, name="top")
-        nc.vector.reduce_max(top[:], w_cols, axis=AXIS.X)
-        shifted = held.tile([P, BLOCKS, GATES], F32, name="shifted")
-        nc.vector.tensor_sub(
-            shifted[:], w_cols, top[:].unsqueeze(2).to_broadcast([P, BLOCKS, GATES])
-        )
+        minus_top = held.tile([P, BLOCKS], F32, name="minus_top")
+        nc.vector.reduce_max(minus_top[:], w_cols, axis=AXIS.X, negate=True)
         weight = held.tile([P, BLOCKS, GATES], F32, name="weight")
-        nc.scalar.activation(weight[:], shifted[:], ACT.Exp)
-
         total = held.tile([P, BLOCKS, 1], F32, name="total")
-        nc.vector.reduce_sum(total[:], weight[:], axis=AXIS.X)
+        for blk in range(BLOCKS):
+            nc.scalar.activation(
+                weight[:, blk, :],
+                w_cols[:, blk, :],
+                ACT.Exp,
+                bias=minus_top[:, blk : blk + 1],
+                accum_out=total[:, blk, :],
+            )
+
         r_col = held.tile([P, BLOCKS, 1], F32, name="r_col")
         nc.vector.reciprocal(r_col[:], total[:])
         shape = [P, BLOCKS, COEFS, GATES]
@@ -72,8 +74,9 @@ def tile_tanklogicvaluenetwork_kernel(tc, x, w, offs, out):
         nc.vector.tensor_mul(k_col[:], n_col[:, :, 0:2], r_col[:].to_broadcast([P, BLOCKS, 2]))
 
         def as_row(name, columns):
-            bank = psum.tile([P, NEURONS], F32, name=name)
-            for blk in range(BLOCKS):
+            blocks = columns.shape[1]
+            bank = psum.tile([P, blocks * P], F32, name=name)
+            for blk in range(blocks):
                 nc.tensor.transpose(
                     bank[:, blk * P : (blk + 1) * P],
                     columns[:, blk : blk + 1].to_broadcast([P, P]),
@@ -81,7 +84,10 @@ def tile_tanklogicvaluenetwork_kernel(tc, x, w, offs, out):
                 )
             return bank
 
-        r_bank = as_row("r_bank", r_col[:, :, 0])
+        r_banks = [
+            as_row("r_bank%d" % h, r_col[:, h * BLOCKS // 2 : (h + 1) * BLOCKS // 2, 0])
+            for h in range(2)
+        ]
         n3_bank = as_row("n3_bank", n_col[:, :, 3])
         n2_bank = as_row("n2_bank", n_col[:, :, 2])
         k1_bank = as_row("k1_bank", k_col[:, :, 1])
@@ -99,8 +105,8 @@ def tile_tanklogicvaluenetwork_kernel(tc, x, w, offs, out):
             start = (first_entry + half.start) // 16
             return offsets[:, start : start + HALF // 16]
 
-        for half in halves:
-            nc.vector.tensor_copy(r_rows[:, half], r_bank[:, half])
+        for half, r_bank in zip(halves, r_banks):
+            nc.scalar.copy(r_rows[:, half], r_bank[:])
         for half in halves:
             second_inputs = table[:].indirect(list_columns(NEURONS, half))
             nc.vector.tensor_tensor(r_b[:, half], second_inputs, r_rows[:, half], ALU.mult)

@@ -50,17 +50,18 @@ def tile_tanklogicvaluenetwork_kernel(tc, x, w, offs, out):
         nc.vector.reduce_max(minus_top[:], w_cols, axis=AXIS.X, negate=True)
         weight = held.tile([P, BLOCKS, GATES], F32, name="weight")
         total = held.tile([P, BLOCKS, 1], F32, name="total")
-        for blk in range(BLOCKS):
-            nc.scalar.activation(
-                weight[:, blk, :],
-                w_cols[:, blk, :],
-                ACT.Exp,
-                bias=minus_top[:, blk : blk + 1],
-                accum_out=total[:, blk, :],
-            )
-
         r_col = held.tile([P, BLOCKS, 1], F32, name="r_col")
-        nc.vector.reciprocal(r_col[:], total[:])
+        for h in range(2):
+            blocks_of_half = slice(h * BLOCKS // 2, (h + 1) * BLOCKS // 2)
+            for blk in range(blocks_of_half.start, blocks_of_half.stop):
+                nc.scalar.activation(
+                    weight[:, blk, :],
+                    w_cols[:, blk, :],
+                    ACT.Exp,
+                    bias=minus_top[:, blk : blk + 1],
+                    accum_out=total[:, blk, :],
+                )
+            nc.vector.reciprocal(r_col[:, blocks_of_half, :], total[:, blocks_of_half, :])
         shape = [P, BLOCKS, COEFS, GATES]
         weighted = held.tile(shape, F32, name="weighted")
         nc.vector.tensor_mul(
@@ -88,15 +89,27 @@ def tile_tanklogicvaluenetwork_kernel(tc, x, w, offs, out):
             as_row("r_bank%d" % h, r_col[:, h * BLOCKS // 2 : (h + 1) * BLOCKS // 2, 0])
             for h in range(2)
         ]
-        n3_bank = as_row("n3_bank", n_col[:, :, 3])
         n2_bank = as_row("n2_bank", n_col[:, :, 2])
+        n3_bank = as_row("n3_bank", n_col[:, :, 3])
         k1_bank = as_row("k1_bank", k_col[:, :, 1])
-        k0_bank = as_row("k0_bank", k_col[:, :, 0])
+        base_banks = []
+        for h in range(2):
+            base_bank = psum.tile([P, HALF], F32, name="base_bank%d" % h)
+            for i in range(HALF // P):
+                nc.tensor.matmul(
+                    base_bank[:, i * P : (i + 1) * P],
+                    lhsT=k_col[:, h * HALF // P + i, 0:1].to_broadcast([P, P]),
+                    rhs=identity[:],
+                    is_transpose=True,
+                    start=(i == 0),
+                    stop=False,
+                )
+            base_banks.append(base_bank)
 
         r_rows = held.tile([P, NEURONS], F32, name="r_rows")
         r_b = held.tile([P, NEURONS], F32, name="r_b")
         slope = held.tile([P, NEURONS], F32, name="slope")
-        base = held.tile([P, NEURONS], F32, name="base")
+        k2_b = held.tile([P, NEURONS], F32, name="k2_b")
         a_slope = held.tile([P, NEURONS], F32, name="a_slope")
         result = held.tile([P, NEURONS], F32, name="result")
         halves = [slice(h * HALF, (h + 1) * HALF) for h in range(2)]
@@ -110,17 +123,18 @@ def tile_tanklogicvaluenetwork_kernel(tc, x, w, offs, out):
         for half in halves:
             second_inputs = table[:].indirect(list_columns(NEURONS, half))
             nc.vector.tensor_tensor(r_b[:, half], second_inputs, r_rows[:, half], ALU.mult)
+        for half, base_bank in zip(halves, base_banks):
+            nc.vector.tensor_mul(k2_b[:, half], r_b[:, half], n2_bank[:, half])
+            nc.tensor.matmul(
+                base_bank[:], lhsT=identity[:], rhs=k2_b[:, half], start=False, stop=True
+            )
         for half in halves:
             nc.vector.tensor_mul(slope[:, half], r_b[:, half], n3_bank[:, half])
         for half in halves:
-            nc.vector.tensor_mul(base[:, half], r_b[:, half], n2_bank[:, half])
-        for half in halves:
             nc.vector.tensor_add(slope[:, half], slope[:, half], k1_bank[:, half])
-        for half in halves:
-            nc.vector.tensor_add(base[:, half], base[:, half], k0_bank[:, half])
         for half in halves:
             first_inputs = table[:].indirect(list_columns(0, half))
             nc.vector.tensor_tensor(a_slope[:, half], first_inputs, slope[:, half], ALU.mult)
-        for half in halves:
-            nc.vector.tensor_add(result[:, half], a_slope[:, half], base[:, half])
+        for half, base_bank in zip(halves, base_banks):
+            nc.vector.tensor_add(result[:, half], a_slope[:, half], base_bank[:])
             nc.sync.dma_start(out[:, half], result[:, half])

@@ -43,17 +43,18 @@ def tile_tanklogicvaluenetwork_kernel(tc, x, w, offs, out):
         nc.vector.tensor_sub(gate[:, 1:3, :], gate[:, 1:3, :], bit3_twice)
         nc.vector.tensor_sub(gate[:, 3, :], gate[:, 3, :], gate[:, 2, :])
 
-        w_bank = psum.tile([P, GATES * BLOCKS], F32, name="w_bank")
-        nc.tensor.transpose(w_bank[:], w_rows[:], identity[0 : GATES * BLOCKS, 0 : GATES * BLOCKS])
-        w_cols = w_bank[:].rearrange("p (q blk) -> p blk q", blk=BLOCKS)
+        w_bank = psum.tile([P, 2 * P], F32, name="w_bank")
+        w_turned = w_bank[:, 0 : GATES * BLOCKS]
+        nc.tensor.transpose(w_turned, w_rows[:], identity[0 : GATES * BLOCKS, 0 : GATES * BLOCKS])
+        w_cols = w_turned.rearrange("p (q blk) -> p blk q", blk=BLOCKS)
         minus_top = held.tile([P, BLOCKS], F32, name="minus_top")
         nc.vector.reduce_max(minus_top[:], w_cols, axis=AXIS.X, negate=True)
         weight = held.tile([P, BLOCKS, GATES], F32, name="weight")
         total = held.tile([P, BLOCKS, 1], F32, name="total")
+        r_pieces = [slice(0, 1), slice(1, 2), slice(2, BLOCKS)]
         r_col = held.tile([P, BLOCKS, 1], F32, name="r_col")
-        for h in range(2):
-            blocks_of_half = slice(h * BLOCKS // 2, (h + 1) * BLOCKS // 2)
-            for blk in range(blocks_of_half.start, blocks_of_half.stop):
+        for piece in r_pieces:
+            for blk in range(piece.start, piece.stop):
                 nc.scalar.activation(
                     weight[:, blk, :],
                     w_cols[:, blk, :],
@@ -61,73 +62,81 @@ def tile_tanklogicvaluenetwork_kernel(tc, x, w, offs, out):
                     bias=minus_top[:, blk : blk + 1],
                     accum_out=total[:, blk, :],
                 )
-            nc.vector.reciprocal(r_col[:, blocks_of_half, :], total[:, blocks_of_half, :])
+            nc.vector.reciprocal(r_col[:, piece, :], total[:, piece, :])
+        block_halves = [slice(h * BLOCKS // 2, (h + 1) * BLOCKS // 2) for h in range(2)]
         shape = [P, BLOCKS, COEFS, GATES]
         weighted = held.tile(shape, F32, name="weighted")
+        n_col = held.tile([P, BLOCKS, COEFS], F32, name="n_col")
+        k_col = held.tile([P, BLOCKS, 2], F32, name="k_col")
         nc.vector.tensor_mul(
             weighted[:],
             weight[:].unsqueeze(2).to_broadcast(shape),
             gate[:].unsqueeze(1).to_broadcast(shape),
         )
-        n_col = held.tile([P, BLOCKS, COEFS], F32, name="n_col")
         nc.vector.reduce_sum(n_col[:], weighted[:], axis=AXIS.X)
-        k_col = held.tile([P, BLOCKS, 2], F32, name="k_col")
         nc.vector.tensor_mul(k_col[:], n_col[:, :, 0:2], r_col[:].to_broadcast([P, BLOCKS, 2]))
 
-        def as_row(name, columns):
-            blocks = columns.shape[1]
-            bank = psum.tile([P, blocks * P], F32, name=name)
-            for blk in range(blocks):
+        def as_rows(name, columns, tag=None):
+            bank = psum.tile([P, len(columns) * P], F32, name=name, tag=tag or name)
+            for i, column in enumerate(columns):
                 nc.tensor.transpose(
-                    bank[:, blk * P : (blk + 1) * P],
-                    columns[:, blk : blk + 1].to_broadcast([P, P]),
-                    identity[:],
+                    bank[:, i * P : (i + 1) * P], column.to_broadcast([P, P]), identity[:]
                 )
             return bank
 
+        def blocks_in(some):
+            return range(some.start, some.stop)
+
+        piece_tags = ["piece0", "piece1", "w_bank"]
         r_banks = [
-            as_row("r_bank%d" % h, r_col[:, h * BLOCKS // 2 : (h + 1) * BLOCKS // 2, 0])
-            for h in range(2)
+            as_rows("r_bank%d" % i, [r_col[:, blk, :] for blk in blocks_in(piece)], tag=tag)
+            for i, (piece, tag) in enumerate(zip(r_pieces, piece_tags))
         ]
-        n2_bank = as_row("n2_bank", n_col[:, :, 2])
-        n3_bank = as_row("n3_bank", n_col[:, :, 3])
-        k1_bank = as_row("k1_bank", k_col[:, :, 1])
-        base_banks = []
-        for h in range(2):
-            base_bank = psum.tile([P, HALF], F32, name="base_bank%d" % h)
-            for i in range(HALF // P):
-                nc.tensor.matmul(
-                    base_bank[:, i * P : (i + 1) * P],
-                    lhsT=k_col[:, h * HALF // P + i, 0:1].to_broadcast([P, P]),
-                    rhs=identity[:],
-                    is_transpose=True,
-                    start=(i == 0),
-                    stop=False,
-                )
-            base_banks.append(base_bank)
+        n3_bank = as_rows("n3_bank", [n_col[:, blk, 3:4] for blk in range(BLOCKS)])
+        k1_bank = as_rows("k1_bank", [k_col[:, blk, 1:2] for blk in range(BLOCKS)])
 
         r_rows = held.tile([P, NEURONS], F32, name="r_rows")
         r_b = held.tile([P, NEURONS], F32, name="r_b")
+        base_turned = held.tile([P, BLOCKS, P], F32, name="base_turned")
         slope = held.tile([P, NEURONS], F32, name="slope")
-        k2_b = held.tile([P, NEURONS], F32, name="k2_b")
         a_slope = held.tile([P, NEURONS], F32, name="a_slope")
         result = held.tile([P, NEURONS], F32, name="result")
         halves = [slice(h * HALF, (h + 1) * HALF) for h in range(2)]
 
-        def list_columns(first_entry, half):
-            start = (first_entry + half.start) // 16
-            return offsets[:, start : start + HALF // 16]
+        def list_columns(first_entry, neurons):
+            return offsets[:, (first_entry + neurons.start) // 16 : (first_entry + neurons.stop) // 16]
 
-        for half, r_bank in zip(halves, r_banks):
-            nc.scalar.copy(r_rows[:, half], r_bank[:])
-        for half in halves:
-            second_inputs = table[:].indirect(list_columns(NEURONS, half))
-            nc.vector.tensor_tensor(r_b[:, half], second_inputs, r_rows[:, half], ALU.mult)
-        for half, base_bank in zip(halves, base_banks):
-            nc.vector.tensor_mul(k2_b[:, half], r_b[:, half], n2_bank[:, half])
-            nc.tensor.matmul(
-                base_bank[:], lhsT=identity[:], rhs=k2_b[:, half], start=False, stop=True
+        for piece, r_bank in zip(r_pieces, r_banks):
+            neurons = slice(piece.start * P, piece.stop * P)
+            nc.scalar.copy(r_rows[:, neurons], r_bank[:])
+            second_inputs = table[:].indirect(list_columns(NEURONS, neurons))
+            nc.vector.tensor_tensor(r_b[:, neurons], second_inputs, r_rows[:, neurons], ALU.mult)
+
+        for piece, tag in zip(r_pieces, piece_tags):
+            r_b_turned = psum.tile(
+                [P, (piece.stop - piece.start) * P], F32, name="r_b_turned_" + tag, tag=tag
             )
+            for i, blk in enumerate(blocks_in(piece)):
+                nc.tensor.transpose(
+                    r_b_turned[:, i * P : (i + 1) * P], r_b[:, blk * P : (blk + 1) * P], identity[:]
+                )
+            for i, blk in enumerate(blocks_in(piece)):
+                nc.scalar.activation(
+                    base_turned[:, blk, :],
+                    r_b_turned[:, i * P : (i + 1) * P],
+                    ACT.Identity,
+                    bias=k_col[:, blk, 0:1],
+                    scale=n_col[:, blk, 2:3],
+                )
+        base_banks = []
+        for h, blocks in enumerate(block_halves):
+            base_bank = psum.tile([P, HALF], F32, name="base_bank%d" % h)
+            for i, blk in enumerate(blocks_in(blocks)):
+                nc.tensor.transpose(
+                    base_bank[:, i * P : (i + 1) * P], base_turned[:, blk, :], identity[:]
+                )
+            base_banks.append(base_bank)
+
         for half in halves:
             nc.vector.tensor_mul(slope[:, half], r_b[:, half], n3_bank[:, half])
         for half in halves:

@@ -28,7 +28,8 @@ def tile_tanklogicvaluenetwork_kernel(tc, x, w, offs, out):
         offsets = held.tile([P, 2 * LIST_COLS], U16, name="offsets")
         nc.sync.dma_start(offsets[:], offs)
         table = held.tile([P, INPUTS], F32, name="table")
-        nc.sync.dma_start(table[:], x)
+        nc.scalar.dma_start(table[:, 0 : INPUTS // 2], x[:, 0 : INPUTS // 2])
+        nc.sync.dma_start(table[:, INPUTS // 2 : INPUTS], x[:, INPUTS // 2 : INPUTS])
 
         identity = held.tile([P, P], F32, name="identity")
         make_identity(nc, identity[:])

@@ -145,6 +145,9 @@ def tile_tanklogicvaluenetwork_kernel(tc, x, w, offs, out):
         for half in halves:
             first_inputs = table[:].indirect(list_columns(0, half))
             nc.vector.tensor_tensor(a_slope[:, half], first_inputs, slope[:, half], ALU.mult)
-        for half, base_bank in zip(halves, base_banks):
-            nc.vector.tensor_add(result[:, half], a_slope[:, half], base_bank[:])
-            nc.sync.dma_start(out[:, half], result[:, half])
+        for blk in range(BLOCKS):
+            neurons = slice(blk * P, (blk + 1) * P)
+            in_bank = slice(neurons.start % HALF, neurons.start % HALF + P)
+            base_bank = base_banks[neurons.start // HALF]
+            nc.vector.tensor_add(result[:, neurons], a_slope[:, neurons], base_bank[:, in_bank])
+            nc.sync.dma_start(out[:, neurons], result[:, neurons])

@@ -16,6 +16,9 @@ LIST_COLS = NEURONS // 16
 COEFS = 4
 HALF = NEURONS // 2
 
+UNIT = 2.0**100
+SHIFT = UNIT * 2.0**-150
+
 
 def tile_tanklogicvaluenetwork_kernel(tc, x, w, offs, out):
     nc = tc.nc
@@ -43,6 +46,10 @@ def tile_tanklogicvaluenetwork_kernel(tc, x, w, offs, out):
         nc.vector.tensor_sub(gate[:, 3, :], gate[:, 3, :], gate[:, 1, :])
         nc.vector.tensor_sub(gate[:, 1:3, :], gate[:, 1:3, :], bit3_twice)
         nc.vector.tensor_sub(gate[:, 3, :], gate[:, 3, :], gate[:, 2, :])
+        gate3_and_shift = held.tile([P, GATES + 1], F32, name="gate3_and_shift")
+        nc.vector.memset(gate3_and_shift[:], SHIFT)
+        nc.vector.tensor_scalar_mul(gate3_and_shift[:, 0:GATES], gate[:, 3, :], UNIT)
+        nc.vector.tensor_scalar_mul(gate[:, 1, :], gate[:, 1, :], UNIT)
 
         w_bank = psum.tile([P, 2 * P], F32, name="w_bank")
         w_turned = w_bank[:, 0 : GATES * BLOCKS]
@@ -50,11 +57,15 @@ def tile_tanklogicvaluenetwork_kernel(tc, x, w, offs, out):
         w_cols = w_turned.rearrange("p (q blk) -> p blk q", blk=BLOCKS)
         minus_top = held.tile([P, BLOCKS], F32, name="minus_top")
         nc.vector.reduce_max(minus_top[:], w_cols, axis=AXIS.X, negate=True)
-        weight = held.tile([P, BLOCKS, GATES], F32, name="weight")
+        weight_and_1 = held.tile([P, BLOCKS, GATES + 1], F32, name="weight_and_1")
+        nc.vector.memset(weight_and_1[:], 1.0)
+        weight = weight_and_1[:, :, 0:GATES]
         total = held.tile([P, BLOCKS, 1], F32, name="total")
-        r_pieces = [slice(0, 1), slice(1, 2), slice(2, BLOCKS)]
+        pieces = [slice(0, 1), slice(1, 2), slice(2, BLOCKS)]
         r_col = held.tile([P, BLOCKS, 1], F32, name="r_col")
-        for piece in r_pieces:
+        weighted3 = held.tile([P, BLOCKS, GATES + 1], F32, name="weighted3")
+        k3_col = held.tile([P, BLOCKS, 1], F32, name="k3_col")
+        for piece in pieces:
             for blk in range(piece.start, piece.stop):
                 nc.scalar.activation(
                     weight[:, blk, :],
@@ -64,18 +75,32 @@ def tile_tanklogicvaluenetwork_kernel(tc, x, w, offs, out):
                     accum_out=total[:, blk, :],
                 )
             nc.vector.reciprocal(r_col[:, piece, :], total[:, piece, :])
+            for blk in range(piece.start, piece.stop):
+                nc.vector.scalar_tensor_tensor(
+                    weighted3[:, blk, :],
+                    weight_and_1[:, blk, :],
+                    r_col[:, blk, :],
+                    gate3_and_shift[:],
+                    ALU.mult,
+                    ALU.mult,
+                    accum_out=k3_col[:, blk, :],
+                )
         block_halves = [slice(h * BLOCKS // 2, (h + 1) * BLOCKS // 2) for h in range(2)]
-        shape = [P, BLOCKS, COEFS, GATES]
+        shape = [P, BLOCKS, 3, GATES]
         weighted = held.tile(shape, F32, name="weighted")
-        n_col = held.tile([P, BLOCKS, COEFS], F32, name="n_col")
-        k_col = held.tile([P, BLOCKS, 2], F32, name="k_col")
+        n_col = held.tile([P, BLOCKS, 3], F32, name="n_col")
+        k_col = held.tile([P, BLOCKS, 3], F32, name="k_col")
+        one_by_k3 = held.tile([P, BLOCKS, 1], F32, name="one_by_k3")
+        k2_by_k3 = held.tile([P, BLOCKS, 1], F32, name="k2_by_k3")
         nc.vector.tensor_mul(
             weighted[:],
-            weight[:].unsqueeze(2).to_broadcast(shape),
-            gate[:].unsqueeze(1).to_broadcast(shape),
+            weight.unsqueeze(2).to_broadcast(shape),
+            gate[:, 0:3, :].unsqueeze(1).to_broadcast(shape),
         )
         nc.vector.reduce_sum(n_col[:], weighted[:], axis=AXIS.X)
-        nc.vector.tensor_mul(k_col[:], n_col[:, :, 0:2], r_col[:].to_broadcast([P, BLOCKS, 2]))
+        nc.vector.tensor_mul(k_col[:], n_col[:], r_col[:].to_broadcast([P, BLOCKS, 3]))
+        nc.vector.reciprocal(one_by_k3[:], k3_col[:])
+        nc.vector.tensor_mul(k2_by_k3[:], k_col[:, :, 2:3], one_by_k3[:])
 
         def as_rows(name, columns, tag=None):
             bank = psum.tile([P, len(columns) * P], F32, name=name, tag=tag or name)
@@ -89,15 +114,14 @@ def tile_tanklogicvaluenetwork_kernel(tc, x, w, offs, out):
             return range(some.start, some.stop)
 
         piece_tags = ["piece0", "piece1", "w_bank"]
-        r_banks = [
-            as_rows("r_bank%d" % i, [r_col[:, blk, :] for blk in blocks_in(piece)], tag=tag)
-            for i, (piece, tag) in enumerate(zip(r_pieces, piece_tags))
+        k3_banks = [
+            as_rows("k3_bank%d" % i, [k3_col[:, blk, :] for blk in blocks_in(piece)], tag=tag)
+            for i, (piece, tag) in enumerate(zip(pieces, piece_tags))
         ]
-        n3_bank = as_rows("n3_bank", [n_col[:, blk, 3:4] for blk in range(BLOCKS)])
         k1_bank = as_rows("k1_bank", [k_col[:, blk, 1:2] for blk in range(BLOCKS)])
 
-        r_rows = held.tile([P, NEURONS], F32, name="r_rows")
-        r_b = held.tile([P, NEURONS], F32, name="r_b")
+        k3_rows = held.tile([P, NEURONS], F32, name="k3_rows")
+        k3_b = held.tile([P, NEURONS], F32, name="k3_b")
         base_turned = held.tile([P, BLOCKS, P], F32, name="base_turned")
         slope = held.tile([P, NEURONS], F32, name="slope")
         a_slope = held.tile([P, NEURONS], F32, name="a_slope")
@@ -107,27 +131,27 @@ def tile_tanklogicvaluenetwork_kernel(tc, x, w, offs, out):
         def list_columns(first_entry, neurons):
             return offsets[:, (first_entry + neurons.start) // 16 : (first_entry + neurons.stop) // 16]
 
-        for piece, r_bank in zip(r_pieces, r_banks):
+        for piece, k3_bank in zip(pieces, k3_banks):
             neurons = slice(piece.start * P, piece.stop * P)
-            nc.scalar.copy(r_rows[:, neurons], r_bank[:])
+            nc.scalar.copy(k3_rows[:, neurons], k3_bank[:])
             second_inputs = table[:].indirect(list_columns(NEURONS, neurons))
-            nc.vector.tensor_tensor(r_b[:, neurons], second_inputs, r_rows[:, neurons], ALU.mult)
+            nc.vector.tensor_tensor(k3_b[:, neurons], second_inputs, k3_rows[:, neurons], ALU.mult)
 
-        for piece, tag in zip(r_pieces, piece_tags):
-            r_b_turned = psum.tile(
-                [P, (piece.stop - piece.start) * P], F32, name="r_b_turned_" + tag, tag=tag
+        for piece, tag in zip(pieces, piece_tags):
+            k3_b_turned = psum.tile(
+                [P, (piece.stop - piece.start) * P], F32, name="k3_b_turned_" + tag, tag=tag
             )
             for i, blk in enumerate(blocks_in(piece)):
                 nc.tensor.transpose(
-                    r_b_turned[:, i * P : (i + 1) * P], r_b[:, blk * P : (blk + 1) * P], identity[:]
+                    k3_b_turned[:, i * P : (i + 1) * P], k3_b[:, blk * P : (blk + 1) * P], identity[:]
                 )
             for i, blk in enumerate(blocks_in(piece)):
                 nc.scalar.activation(
                     base_turned[:, blk, :],
-                    r_b_turned[:, i * P : (i + 1) * P],
+                    k3_b_turned[:, i * P : (i + 1) * P],
                     ACT.Identity,
                     bias=k_col[:, blk, 0:1],
-                    scale=n_col[:, blk, 2:3],
+                    scale=k2_by_k3[:, blk, :],
                 )
         base_banks = []
         for h, blocks in enumerate(block_halves):
@@ -139,9 +163,7 @@ def tile_tanklogicvaluenetwork_kernel(tc, x, w, offs, out):
             base_banks.append(base_bank)
 
         for half in halves:
-            nc.vector.tensor_mul(slope[:, half], r_b[:, half], n3_bank[:, half])
-        for half in halves:
-            nc.vector.tensor_add(slope[:, half], slope[:, half], k1_bank[:, half])
+            nc.vector.tensor_add(slope[:, half], k3_b[:, half], k1_bank[:, half])
         for half in halves:
             first_inputs = table[:].indirect(list_columns(0, half))
             nc.vector.tensor_tensor(a_slope[:, half], first_inputs, slope[:, half], ALU.mult)
@@ -149,5 +171,7 @@ def tile_tanklogicvaluenetwork_kernel(tc, x, w, offs, out):
             neurons = slice(blk * P, (blk + 1) * P)
             in_bank = slice(neurons.start % HALF, neurons.start % HALF + P)
             base_bank = base_banks[neurons.start // HALF]
-            nc.vector.tensor_add(result[:, neurons], a_slope[:, neurons], base_bank[:, in_bank])
+            nc.vector.scalar_tensor_tensor(
+                result[:, neurons], a_slope[:, neurons], 1 / UNIT, base_bank[:, in_bank], ALU.mult, ALU.add
+            )
             nc.sync.dma_start(out[:, neurons], result[:, neurons])

@@ -79,7 +79,7 @@ def tile_tanklogicvaluenetwork_kernel(tc, x, w, offs, out):
                 nc.vector.scalar_tensor_tensor(
                     weighted3[:, blk, :],
                     weight_and_1[:, blk, :],
-                    r_col[:, blk, :],
+                    1.0 if blk == 0 else r_col[:, blk, :],
                     gate3_and_shift[:],
                     ALU.mult,
                     ALU.mult,
@@ -90,8 +90,8 @@ def tile_tanklogicvaluenetwork_kernel(tc, x, w, offs, out):
         weighted = held.tile(shape, F32, name="weighted")
         n_col = held.tile([P, BLOCKS, 3], F32, name="n_col")
         k_col = held.tile([P, BLOCKS, 3], F32, name="k_col")
-        one_by_k3 = held.tile([P, BLOCKS, 1], F32, name="one_by_k3")
-        k2_by_k3 = held.tile([P, BLOCKS, 1], F32, name="k2_by_k3")
+        one_by_k3 = held.tile([P, BLOCKS - 1, 1], F32, name="one_by_k3")
+        k2_by_k3 = held.tile([P, BLOCKS - 1, 1], F32, name="k2_by_k3")
         nc.vector.tensor_mul(
             weighted[:],
             weight.unsqueeze(2).to_broadcast(shape),
@@ -99,8 +99,9 @@ def tile_tanklogicvaluenetwork_kernel(tc, x, w, offs, out):
         )
         nc.vector.reduce_sum(n_col[:], weighted[:], axis=AXIS.X)
         nc.vector.tensor_mul(k_col[:], n_col[:], r_col[:].to_broadcast([P, BLOCKS, 3]))
-        nc.vector.reciprocal(one_by_k3[:], k3_col[:])
-        nc.vector.tensor_mul(k2_by_k3[:], k_col[:, :, 2:3], one_by_k3[:])
+        nc.vector.reciprocal(one_by_k3[:], k3_col[:, 1:BLOCKS, :])
+        nc.vector.tensor_mul(k2_by_k3[:], k_col[:, 1:BLOCKS, 2:3], one_by_k3[:])
+        k2_by_factor = [n_col[:, 0, 2:3]] + [k2_by_k3[:, i, :] for i in range(BLOCKS - 1)]
 
         def as_rows(name, columns, tag=None):
             bank = psum.tile([P, len(columns) * P], F32, name=name, tag=tag or name)
@@ -114,13 +115,16 @@ def tile_tanklogicvaluenetwork_kernel(tc, x, w, offs, out):
             return range(some.start, some.stop)
 
         piece_tags = ["piece0", "piece1", "w_bank"]
-        k3_banks = [
-            as_rows("k3_bank%d" % i, [k3_col[:, blk, :] for blk in blocks_in(piece)], tag=tag)
+        factor_col = [r_col[:, 0, :]] + [k3_col[:, blk, :] for blk in range(1, BLOCKS)]
+        factor_banks = [
+            as_rows("factor_bank%d" % i, [factor_col[blk] for blk in blocks_in(piece)], tag=tag)
             for i, (piece, tag) in enumerate(zip(pieces, piece_tags))
         ]
+        n3_bank = as_rows("n3_bank", [k3_col[:, 0, :]])
         k1_bank = as_rows("k1_bank", [k_col[:, blk, 1:2] for blk in range(BLOCKS)])
 
-        k3_rows = held.tile([P, NEURONS], F32, name="k3_rows")
+        factor_rows = held.tile([P, NEURONS], F32, name="factor_rows")
+        r_b = held.tile([P, P], F32, name="r_b")
         k3_b = held.tile([P, NEURONS], F32, name="k3_b")
         base_turned = held.tile([P, BLOCKS, P], F32, name="base_turned")
         slope = held.tile([P, NEURONS], F32, name="slope")
@@ -131,27 +135,26 @@ def tile_tanklogicvaluenetwork_kernel(tc, x, w, offs, out):
         def list_columns(first_entry, neurons):
             return offsets[:, (first_entry + neurons.start) // 16 : (first_entry + neurons.stop) // 16]
 
-        for piece, k3_bank in zip(pieces, k3_banks):
+        for i, (piece, factor_bank) in enumerate(zip(pieces, factor_banks)):
             neurons = slice(piece.start * P, piece.stop * P)
-            nc.scalar.copy(k3_rows[:, neurons], k3_bank[:])
+            nc.scalar.copy(factor_rows[:, neurons], factor_bank[:])
             second_inputs = table[:].indirect(list_columns(NEURONS, neurons))
-            nc.vector.tensor_tensor(k3_b[:, neurons], second_inputs, k3_rows[:, neurons], ALU.mult)
+            product = r_b[:] if i == 0 else k3_b[:, neurons]
+            nc.vector.tensor_tensor(product, second_inputs, factor_rows[:, neurons], ALU.mult)
+        nc.vector.tensor_mul(k3_b[:, 0:P], r_b[:], n3_bank[:])
 
         for piece, tag in zip(pieces, piece_tags):
-            k3_b_turned = psum.tile(
-                [P, (piece.stop - piece.start) * P], F32, name="k3_b_turned_" + tag, tag=tag
-            )
+            turned = psum.tile([P, (piece.stop - piece.start) * P], F32, name="turned_" + tag, tag=tag)
             for i, blk in enumerate(blocks_in(piece)):
-                nc.tensor.transpose(
-                    k3_b_turned[:, i * P : (i + 1) * P], k3_b[:, blk * P : (blk + 1) * P], identity[:]
-                )
+                product = r_b[:] if blk == 0 else k3_b[:, blk * P : (blk + 1) * P]
+                nc.tensor.transpose(turned[:, i * P : (i + 1) * P], product, identity[:])
             for i, blk in enumerate(blocks_in(piece)):
                 nc.scalar.activation(
                     base_turned[:, blk, :],
-                    k3_b_turned[:, i * P : (i + 1) * P],
+                    turned[:, i * P : (i + 1) * P],
                     ACT.Identity,
                     bias=k_col[:, blk, 0:1],
-                    scale=k2_by_k3[:, blk, :],
+                    scale=k2_by_factor[blk],
                 )
         base_banks = []
         for h, blocks in enumerate(block_halves):

import concourse.mybir as mybir
from concourse.masks import make_identity

F32 = mybir.dt.float32
U16 = mybir.dt.uint16
ALU = mybir.AluOpType
ACT = mybir.ActivationFunctionType
AXIS = mybir.AxisListType

P = 128
INPUTS = 2048
NEURONS = 512
GATES = 16
BLOCKS = NEURONS // P
LIST_COLS = NEURONS // 16
COEFS = 4
HALF = NEURONS // 2

UNIT = 2.0**100
SHIFT = UNIT * 2.0**-150


def tile_tanklogicvaluenetwork_kernel(tc, x, w, offs, out):
    nc = tc.nc
    with (
        tc.tile_pool(name="held", bufs=1) as held,
        tc.psum_pool(name="psum", bufs=1) as psum,
    ):
        w_rows = held.tile([GATES * BLOCKS, P], F32, name="w_rows")
        nc.sync.dma_start(w_rows[:], w.rearrange("q (blk n) -> (q blk) n", n=P))
        offsets = held.tile([P, 2 * LIST_COLS], U16, name="offsets")
        nc.sync.dma_start(offsets[:], offs)
        table = held.tile([P, INPUTS], F32, name="table")
        nc.scalar.dma_start(table[:, 0 : INPUTS // 2], x[:, 0 : INPUTS // 2])
        nc.sync.dma_start(table[:, INPUTS // 2 : INPUTS], x[:, INPUTS // 2 : INPUTS])

        identity = held.tile([P, P], F32, name="identity")
        make_identity(nc, identity[:])

        gate = held.tile([P, COEFS, GATES], F32, name="gate")
        nc.vector.memset(gate[:], 0.0)
        for row, bit in ((0, 3), (1, 1), (2, 2), (3, 0)):
            where_set = gate[:, row, :].rearrange("p (h two f) -> p h two f", two=2, f=2**bit)
            nc.vector.memset(where_set[:, :, 1, :], 1.0)
        bit3_twice = gate[:, 0:1, :].to_broadcast([P, 2, GATES])
        nc.vector.tensor_sub(gate[:, 3, :], gate[:, 3, :], gate[:, 1, :])
        nc.vector.tensor_sub(gate[:, 1:3, :], gate[:, 1:3, :], bit3_twice)
        nc.vector.tensor_sub(gate[:, 3, :], gate[:, 3, :], gate[:, 2, :])
        gate3_and_shift = held.tile([P, GATES + 1], F32, name="gate3_and_shift")
        nc.vector.memset(gate3_and_shift[:], SHIFT)
        nc.vector.tensor_scalar_mul(gate3_and_shift[:, 0:GATES], gate[:, 3, :], UNIT)
        nc.vector.tensor_scalar_mul(gate[:, 1, :], gate[:, 1, :], UNIT)

        w_bank = psum.tile([P, 2 * P], F32, name="w_bank")
        w_turned = w_bank[:, 0 : GATES * BLOCKS]
        nc.tensor.transpose(w_turned, w_rows[:], identity[0 : GATES * BLOCKS, 0 : GATES * BLOCKS])
        w_cols = w_turned.rearrange("p (q blk) -> p blk q", blk=BLOCKS)
        minus_top = held.tile([P, BLOCKS], F32, name="minus_top")
        nc.vector.reduce_max(minus_top[:], w_cols, axis=AXIS.X, negate=True)
        weight_and_1 = held.tile([P, BLOCKS, GATES + 1], F32, name="weight_and_1")
        nc.vector.memset(weight_and_1[:], 1.0)
        weight = weight_and_1[:, :, 0:GATES]
        total = held.tile([P, BLOCKS, 1], F32, name="total")
        pieces = [slice(0, 1), slice(1, 2), slice(2, BLOCKS)]
        r_col = held.tile([P, BLOCKS, 1], F32, name="r_col")
        weighted3 = held.tile([P, BLOCKS, GATES + 1], F32, name="weighted3")
        k3_col = held.tile([P, BLOCKS, 1], F32, name="k3_col")
        for piece in pieces:
            for blk in range(piece.start, piece.stop):
                nc.scalar.activation(
                    weight[:, blk, :],
                    w_cols[:, blk, :],
                    ACT.Exp,
                    bias=minus_top[:, blk : blk + 1],
                    accum_out=total[:, blk, :],
                )
            nc.vector.reciprocal(r_col[:, piece, :], total[:, piece, :])
            for blk in range(piece.start, piece.stop):
                nc.vector.scalar_tensor_tensor(
                    weighted3[:, blk, :],
                    weight_and_1[:, blk, :],
                    1.0 if blk == 0 else r_col[:, blk, :],
                    gate3_and_shift[:],
                    ALU.mult,
                    ALU.mult,
                    accum_out=k3_col[:, blk, :],
                )
        block_halves = [slice(h * BLOCKS // 2, (h + 1) * BLOCKS // 2) for h in range(2)]
        shape = [P, BLOCKS, 3, GATES]
        weighted = held.tile(shape, F32, name="weighted")
        n_col = held.tile([P, BLOCKS, 3], F32, name="n_col")
        k_col = held.tile([P, BLOCKS, 3], F32, name="k_col")
        one_by_k3 = held.tile([P, BLOCKS - 1, 1], F32, name="one_by_k3")
        k2_by_k3 = held.tile([P, BLOCKS - 1, 1], F32, name="k2_by_k3")
        nc.vector.tensor_mul(
            weighted[:],
            weight.unsqueeze(2).to_broadcast(shape),
            gate[:, 0:3, :].unsqueeze(1).to_broadcast(shape),
        )
        nc.vector.reduce_sum(n_col[:], weighted[:], axis=AXIS.X)
        nc.vector.tensor_mul(k_col[:], n_col[:], r_col[:].to_broadcast([P, BLOCKS, 3]))
        nc.vector.reciprocal(one_by_k3[:], k3_col[:, 1:BLOCKS, :])
        nc.vector.tensor_mul(k2_by_k3[:], k_col[:, 1:BLOCKS, 2:3], one_by_k3[:])
        k2_by_factor = [n_col[:, 0, 2:3]] + [k2_by_k3[:, i, :] for i in range(BLOCKS - 1)]

        def as_rows(name, columns, tag=None):
            bank = psum.tile([P, len(columns) * P], F32, name=name, tag=tag or name)
            for i, column in enumerate(columns):
                nc.tensor.transpose(
                    bank[:, i * P : (i + 1) * P], column.to_broadcast([P, P]), identity[:]
                )
            return bank

        def blocks_in(some):
            return range(some.start, some.stop)

        piece_tags = ["piece0", "piece1", "w_bank"]
        factor_col = [r_col[:, 0, :]] + [k3_col[:, blk, :] for blk in range(1, BLOCKS)]
        factor_banks = [
            as_rows("factor_bank%d" % i, [factor_col[blk] for blk in blocks_in(piece)], tag=tag)
            for i, (piece, tag) in enumerate(zip(pieces, piece_tags))
        ]
        n3_bank = as_rows("n3_bank", [k3_col[:, 0, :]])
        k1_bank = as_rows("k1_bank", [k_col[:, blk, 1:2] for blk in range(BLOCKS)])

        factor_rows = held.tile([P, NEURONS], F32, name="factor_rows")
        r_b = held.tile([P, P], F32, name="r_b")
        k3_b = held.tile([P, NEURONS], F32, name="k3_b")
        base_turned = held.tile([P, BLOCKS, P], F32, name="base_turned")
        slope = held.tile([P, NEURONS], F32, name="slope")
        a_slope = held.tile([P, NEURONS], F32, name="a_slope")
        result = held.tile([P, NEURONS], F32, name="result")
        halves = [slice(h * HALF, (h + 1) * HALF) for h in range(2)]

        def list_columns(first_entry, neurons):
            return offsets[:, (first_entry + neurons.start) // 16 : (first_entry + neurons.stop) // 16]

        for i, (piece, factor_bank) in enumerate(zip(pieces, factor_banks)):
            neurons = slice(piece.start * P, piece.stop * P)
            nc.scalar.copy(factor_rows[:, neurons], factor_bank[:])
            second_inputs = table[:].indirect(list_columns(NEURONS, neurons))
            product = r_b[:] if i == 0 else k3_b[:, neurons]
            nc.vector.tensor_tensor(product, second_inputs, factor_rows[:, neurons], ALU.mult)
        nc.vector.tensor_mul(k3_b[:, 0:P], r_b[:], n3_bank[:])

        for piece, tag in zip(pieces, piece_tags):
            turned = psum.tile([P, (piece.stop - piece.start) * P], F32, name="turned_" + tag, tag=tag)
            for i, blk in enumerate(blocks_in(piece)):
                product = r_b[:] if blk == 0 else k3_b[:, blk * P : (blk + 1) * P]
                nc.tensor.transpose(turned[:, i * P : (i + 1) * P], product, identity[:])
            for i, blk in enumerate(blocks_in(piece)):
                nc.scalar.activation(
                    base_turned[:, blk, :],
                    turned[:, i * P : (i + 1) * P],
                    ACT.Identity,
                    bias=k_col[:, blk, 0:1],
                    scale=k2_by_factor[blk],
                )
        base_banks = []
        for h, blocks in enumerate(block_halves):
            base_bank = psum.tile([P, HALF], F32, name="base_bank%d" % h)
            for i, blk in enumerate(blocks_in(blocks)):
                nc.tensor.transpose(
                    base_bank[:, i * P : (i + 1) * P], base_turned[:, blk, :], identity[:]
                )
            base_banks.append(base_bank)

        for half in halves:
            nc.vector.tensor_add(slope[:, half], k3_b[:, half], k1_bank[:, half])
        for half in halves:
            first_inputs = table[:].indirect(list_columns(0, half))
            nc.vector.tensor_tensor(a_slope[:, half], first_inputs, slope[:, half], ALU.mult)
        for blk in range(BLOCKS):
            neurons = slice(blk * P, (blk + 1) * P)
            in_bank = slice(neurons.start % HALF, neurons.start % HALF + P)
            base_bank = base_banks[neurons.start // HALF]
            nc.vector.scalar_tensor_tensor(
                result[:, neurons], a_slope[:, neurons], 1 / UNIT, base_bank[:, in_bank], ALU.mult, ALU.add
            )
            nc.sync.dma_start(out[:, neurons], result[:, neurons])
